import numpy as np
import ml_dtypes


def mxq(x, axis, fmt="e4m3"):
    dtype, down = {"e4m3": (ml_dtypes.float8_e4m3fn, 7), "e5m2": (ml_dtypes.float8_e5m2, 14)}[fmt]
    v = np.moveaxis(np.asarray(x, np.float32).astype(ml_dtypes.bfloat16).astype(np.float64), axis, -1)
    blocks = v.reshape(v.shape[:-1] + (-1, 32))
    amax = np.abs(blocks).max(-1, keepdims=True)
    byte = np.maximum(np.where(amax > 0, np.frexp(amax)[1] - 1 + 127, 0) - down, 1)
    scale = np.exp2(byte - 127.0)
    codes = (blocks / scale).astype(np.float32).astype(dtype).astype(np.float64)
    return np.moveaxis((codes * scale).reshape(v.shape), -1, axis)


WIDE = False


def mx_kscale(k):
    if not WIDE:
        return np.ones(k)
    levels = np.array([20, -20, 10, -10, 0])
    a = np.random.permutation(np.resize(levels, k // 512 * 4)).reshape(k // 512, 4)
    idx = np.arange(k)
    return np.exp2(a[idx // 512, idx % 128 // 32])


BF16 = ml_dtypes.bfloat16


def bf(x):
    return np.asarray(x, np.float32).astype(BF16)


def f64(x):
    return np.asarray(x).astype(np.float64)


B, Nb1, Nw1, Nb2x, Nb2y, Nw2x, Nw2y, R, C = 16384, 2, 8, 4, 2, 16, 16, 16, 2
J1 = Nb1 * Nb1
K1 = C * Nw1 * Nw1
J3 = Nb2x * Nb2y
L1 = J3 * R
J2 = J3 * J1


def setup_inputs():
    s = mx_kscale(B)
    x = np.random.standard_normal((B, Nb1, Nw1, Nb1, Nw1, C)) * s[:, None, None, None, None, None]
    k1 = np.random.standard_normal((J1, K1, L1)) / np.sqrt(K1)
    b1 = np.random.standard_normal((1, J1, L1)) * 0.3
    g = np.random.standard_normal((B, J2, R)) * np.exp2(np.random.randint(-12, 1, (B, 1, 1))) / s[:, None, None]
    return {"x": bf(x.reshape(B, Nb1 * Nw1 * Nb1 * Nw1, C)),
            "k1": bf(k1),
            "b1": bf(b1),
            "grad_out": bf(g)}


def reference(x, k1, b1, grad_out):
    h = f64(x).reshape(B, Nb1, Nw1, Nb1, Nw1, C).transpose(0, 1, 3, 2, 4, 5).reshape(B, J1, K1)
    gy = f64(grad_out).reshape(B, R, J1, J3).transpose(0, 2, 3, 1).reshape(B, J1, L1)
    hq = mxq(h, 0, "e4m3").transpose(1, 2, 0)
    gq = mxq(gy, 0, "e5m2").transpose(1, 0, 2)
    return hq @ gq

@@ -1,0 +1,99 @@
+import concourse.mybir as mybir
+
+BF16 = mybir.dt.bfloat16
+F32 = mybir.dt.float32
+U32 = mybir.dt.uint32
+U8 = mybir.dt.uint8
+E4M3_X4 = mybir.dt.float8_e4m3fn_x4
+E5M2_X4 = mybir.dt.float8_e5m2_x4
+
+P = 128
+PACK = 4
+K_PASS = P * PACK
+SAMPLES = 16384
+PASSES = SAMPLES // K_PASS
+WIDTH = 512
+BLOCKS = 4
+WINDOW = 128
+GRID_ROWS = 16
+HALF_ROW = 16
+COEFFS = 16
+OUT_BLOCKS = 8
+RUN = 4
+
+FLOPS = 2 * BLOCKS * WINDOW * (COEFFS * OUT_BLOCKS) * SAMPLES
+BYTES = 2 * SAMPLES * WIDTH * 2 + BLOCKS * WINDOW * COEFFS * OUT_BLOCKS * 4
+
+
+def tile_switchnet_fstar_pa_k_kernel(tc, x, k1, b1, grad_out, out):
+    nc = tc.nc
+
+    x_passes = x.rearrange("(c p t) g ch -> c p (t g ch)", p=P, t=PACK)
+    g_passes = grad_out.rearrange("(c p t) a r -> c p (t a r)", p=P, t=PACK)
+
+    with (
+        tc.tile_pool(name="raw", bufs=6) as raw_pool,
+        tc.tile_pool(name="grouped", bufs=3) as grouped_pool,
+        tc.tile_pool(name="quantised", bufs=3) as quantised_pool,
+        tc.tile_pool(name="result", bufs=1) as result_pool,
+        tc.psum_pool(name="acc", bufs=1) as acc_pool,
+    ):
+        acc = [acc_pool.tile([P, WIDTH], F32, name="acc%d" % j) for j in range(BLOCKS)]
+
+        for c in range(PASSES):
+            raw_g = raw_pool.tile([P, PACK * WIDTH], BF16)
+            nc.sync.dma_start(out=raw_g[:], in_=g_passes[c])
+            raw_x = raw_pool.tile([P, PACK * WIDTH], BF16)
+            nc.sync.dma_start(out=raw_x[:], in_=x_passes[c])
+
+            grouped_g = grouped_pool.tile([P, WIDTH * PACK], BF16, align_bytes=64)
+            nc.scalar.copy(
+                out=grouped_g[:].rearrange("p (w i t) -> p w t i", i=RUN, t=PACK),
+                in_=raw_g[:].rearrange("p (t w i) -> p w t i", t=PACK, i=RUN),
+            )
+            grouped_x = grouped_pool.tile([P, WIDTH * PACK], BF16, align_bytes=64)
+            for block_col in range(2):
+                nc.vector.tensor_copy(
+                    out=grouped_x[:].rearrange(
+                        "p (h row w i t) -> p h row w t i", h=2, row=GRID_ROWS, i=RUN, t=PACK
+                    )[:, block_col],
+                    in_=raw_x[:].rearrange(
+                        "p (t row h w i) -> p h row w t i", t=PACK, row=GRID_ROWS, h=2, i=RUN
+                    )[:, block_col],
+                )
+
+            x_codes = quantised_pool.tile([P, WIDTH], U32, align_bytes=64)
+            x_scales = quantised_pool.tile([P, WIDTH], U8, align_bytes=64)
+            nc.vector.quantize_mx(
+                out=x_codes[:].bitcast(E4M3_X4), scales=x_scales[:], in_=grouped_x[:]
+            )
+            g_codes = quantised_pool.tile([P, WIDTH], U32, align_bytes=64)
+            g_scales = quantised_pool.tile([P, WIDTH], U8, align_bytes=64)
+            nc.vector.quantize_mx(
+                out=g_codes[:].bitcast(E5M2_X4), scales=g_scales[:], in_=grouped_g[:]
+            )
+
+            for j in range(BLOCKS):
+                block_row, block_col = divmod(j, 2)
+                first = (2 * block_col + block_row) * WINDOW
+                nc.tensor.matmul_mx(
+                    out=acc[j][:],
+                    lhsT=x_codes[:, first : first + WINDOW].bitcast(E4M3_X4),
+                    lhsT_scale=x_scales[:, first : first + WINDOW],
+                    rhs=g_codes[:].bitcast(E5M2_X4),
+                    rhs_scale=g_scales[:],
+                    start=(c == 0),
+                    stop=(c == PASSES - 1),
+                )
+
+        result = result_pool.tile([P, BLOCKS, OUT_BLOCKS * COEFFS], F32)
+        for j in range(BLOCKS):
+            picked = acc[j][:].rearrange(
+                "p (r j m) -> p j m r", r=COEFFS, j=BLOCKS, m=OUT_BLOCKS
+            )[:, j]
+            ordered = result[:, j, :].rearrange("p (m r) -> p m r", m=OUT_BLOCKS)
+            if j % 2 == 0:
+                nc.vector.tensor_copy(out=ordered, in_=picked)
+            else:
+                nc.scalar.copy(out=ordered, in_=picked)
+        nc.sync.dma_start(out=out.rearrange("j k l -> k j l"), in_=result[:])

@@ -19,6 +19,8 @@ GRID_ROWS = 16
 HALF_ROW = 16
 COEFFS = 16
 OUT_BLOCKS = 8
+HALF = WIDTH // 2
+HELP_EVERY = 10
 RUN = 4
 
 FLOPS = 2 * BLOCKS * WINDOW * (COEFFS * OUT_BLOCKS) * SAMPLES
@@ -28,10 +30,11 @@ BYTES = 2 * SAMPLES * WIDTH * 2 + BLOCKS * WINDOW * COEFFS * OUT_BLOCKS * 4
 def tile_switchnet_fstar_pa_k_kernel(tc, x, k1, b1, grad_out, out):
     nc = tc.nc
 
-    x_passes = x.rearrange("(c p t) g ch -> c p (t g ch)", p=P, t=PACK)
-    g_passes = grad_out.rearrange("(c p t) a r -> c p (t a r)", p=P, t=PACK)
+    x_view = x.rearrange("(c p t) g ch -> c p t (g ch)", p=P, t=PACK)
+    g_view = grad_out.rearrange("(c p t) a r -> c p t (a r)", p=P, t=PACK)
 
     with (
+        tc.tile_pool(name="first", bufs=1) as first_pool,
         tc.tile_pool(name="raw", bufs=6) as raw_pool,
         tc.tile_pool(name="grouped", bufs=3) as grouped_pool,
         tc.tile_pool(name="quantised", bufs=3) as quantised_pool,
@@ -39,61 +42,85 @@ def tile_switchnet_fstar_pa_k_kernel(tc, x, k1, b1, grad_out, out):
         tc.psum_pool(name="acc", bufs=1) as acc_pool,
     ):
         acc = [acc_pool.tile([P, WIDTH], F32, name="acc%d" % j) for j in range(BLOCKS)]
+        result = result_pool.tile([P, BLOCKS, OUT_BLOCKS * COEFFS], F32)
+
+        def copy_g(engine_copy, grouped_g, source, first_col, cols):
+            engine_copy(
+                out=grouped_g[:, first_col * PACK : (first_col + cols) * PACK].rearrange(
+                    "p (w i t) -> p w t i", i=RUN, t=PACK
+                ),
+                in_=source.rearrange("p t (w i) -> p w t i", i=RUN),
+            )
+
+        def copy_x(engine_copy, grouped_x, source, first_row, rows, h):
+            engine_copy(
+                out=grouped_x[:].rearrange(
+                    "p (h row w i t) -> p h row w t i", h=2, row=GRID_ROWS, i=RUN, t=PACK
+                )[:, h, first_row : first_row + rows],
+                in_=source.rearrange("p t (row h w i) -> p h row w t i", row=rows, h=2, i=RUN)[:, h],
+            )
 
         for c in range(PASSES):
-            raw_g = raw_pool.tile([P, PACK * WIDTH], BF16)
-            nc.sync.dma_start(out=raw_g[:], in_=g_passes[c])
-            raw_x = raw_pool.tile([P, PACK * WIDTH], BF16)
-            nc.sync.dma_start(out=raw_x[:], in_=x_passes[c])
-
             grouped_g = grouped_pool.tile([P, WIDTH * PACK], BF16, align_bytes=64)
-            nc.scalar.copy(
-                out=grouped_g[:].rearrange("p (w i t) -> p w t i", i=RUN, t=PACK),
-                in_=raw_g[:].rearrange("p (t w i) -> p w t i", t=PACK, i=RUN),
-            )
             grouped_x = grouped_pool.tile([P, WIDTH * PACK], BF16, align_bytes=64)
-            for block_col in range(2):
-                nc.vector.tensor_copy(
-                    out=grouped_x[:].rearrange(
-                        "p (h row w i t) -> p h row w t i", h=2, row=GRID_ROWS, i=RUN, t=PACK
-                    )[:, block_col],
-                    in_=raw_x[:].rearrange(
-                        "p (t row h w i) -> p h row w t i", t=PACK, row=GRID_ROWS, h=2, i=RUN
-                    )[:, block_col],
-                )
+            if c == 0:
+                for a in range(2):
+                    cols = slice(a * HALF, (a + 1) * HALF)
+                    half_x = first_pool.tile([P, PACK, HALF], BF16, name="half_x%d" % a)
+                    nc.sync.dma_start(out=half_x[:], in_=x_view[c][:, :, cols])
+                    half_g = first_pool.tile([P, PACK, HALF], BF16, name="half_g%d" % a)
+                    nc.sync.dma_start(out=half_g[:], in_=g_view[c][:, :, cols])
+                    copy_g(nc.scalar.copy, grouped_g, half_g[:], a * HALF, HALF)
+                    for h in range(2):
+                        copy_x(nc.vector.tensor_copy, grouped_x, half_x[:], a * 8, 8, h)
+            else:
+                raw_g = raw_pool.tile([P, PACK, WIDTH], BF16)
+                nc.sync.dma_start(out=raw_g[:], in_=g_view[c])
+                raw_x = raw_pool.tile([P, PACK, WIDTH], BF16)
+                nc.sync.dma_start(out=raw_x[:], in_=x_view[c])
+                copy_g(nc.scalar.copy, grouped_g, raw_g[:], 0, WIDTH)
+                copy_x(nc.vector.tensor_copy, grouped_x, raw_x[:], 0, GRID_ROWS, 0)
+                if c % HELP_EVERY == HELP_EVERY - 1:
+                    copy_x(nc.scalar.copy, grouped_x, raw_x[:], 0, GRID_ROWS, 1)
+                else:
+                    copy_x(nc.vector.tensor_copy, grouped_x, raw_x[:], 0, GRID_ROWS, 1)
 
-            x_codes = quantised_pool.tile([P, WIDTH], U32, align_bytes=64)
-            x_scales = quantised_pool.tile([P, WIDTH], U8, align_bytes=64)
-            nc.vector.quantize_mx(
-                out=x_codes[:].bitcast(E4M3_X4), scales=x_scales[:], in_=grouped_x[:]
-            )
             g_codes = quantised_pool.tile([P, WIDTH], U32, align_bytes=64)
             g_scales = quantised_pool.tile([P, WIDTH], U8, align_bytes=64)
+            x_codes = quantised_pool.tile([P, WIDTH], U32, align_bytes=64)
+            x_scales = quantised_pool.tile([P, WIDTH], U8, align_bytes=64)
+            last = c == PASSES - 1
+            if not last:
+                nc.vector.quantize_mx(
+                    out=x_codes[:].bitcast(E4M3_X4), scales=x_scales[:], in_=grouped_x[:]
+                )
             nc.vector.quantize_mx(
                 out=g_codes[:].bitcast(E5M2_X4), scales=g_scales[:], in_=grouped_g[:]
             )
-
-            for j in range(BLOCKS):
-                block_row, block_col = divmod(j, 2)
-                first = (2 * block_col + block_row) * WINDOW
+            for s in range(BLOCKS):
+                block_col, block_row = divmod(s, 2)
+                j = 2 * block_row + block_col
+                cols = slice(s * WINDOW, (s + 1) * WINDOW)
+                if last:
+                    nc.vector.quantize_mx(
+                        out=x_codes[:, cols].bitcast(E4M3_X4),
+                        scales=x_scales[:, cols],
+                        in_=grouped_x[:, s * WINDOW * PACK : (s + 1) * WINDOW * PACK],
+                    )
                 nc.tensor.matmul_mx(
                     out=acc[j][:],
-                    lhsT=x_codes[:, first : first + WINDOW].bitcast(E4M3_X4),
-                    lhsT_scale=x_scales[:, first : first + WINDOW],
+                    lhsT=x_codes[:, cols].bitcast(E4M3_X4),
+                    lhsT_scale=x_scales[:, cols],
                     rhs=g_codes[:].bitcast(E5M2_X4),
                     rhs_scale=g_scales[:],
                     start=(c == 0),
-                    stop=(c == PASSES - 1),
+                    stop=last,
                 )
-
-        result = result_pool.tile([P, BLOCKS, OUT_BLOCKS * COEFFS], F32)
-        for j in range(BLOCKS):
-            picked = acc[j][:].rearrange(
-                "p (r j m) -> p j m r", r=COEFFS, j=BLOCKS, m=OUT_BLOCKS
-            )[:, j]
-            ordered = result[:, j, :].rearrange("p (m r) -> p m r", m=OUT_BLOCKS)
-            if j % 2 == 0:
-                nc.vector.tensor_copy(out=ordered, in_=picked)
-            else:
-                nc.scalar.copy(out=ordered, in_=picked)
-        nc.sync.dma_start(out=out.rearrange("j k l -> k j l"), in_=result[:])
+                if last:
+                    picked = acc[j][:].rearrange(
+                        "p (r j m) -> p j m r", r=COEFFS, j=BLOCKS, m=OUT_BLOCKS
+                    )[:, j]
+                    nc.scalar.copy(
+                        out=result[:, j, :].rearrange("p (m r) -> p m r", m=OUT_BLOCKS), in_=picked
+                    )
+                    nc.sync.dma_start(out=out[j], in_=result[:, j, :])

@@ -19,8 +19,6 @@ GRID_ROWS = 16
 HALF_ROW = 16
 COEFFS = 16
 OUT_BLOCKS = 8
-HALF = WIDTH // 2
-HELP_EVERY = 10
 RUN = 4
 
 FLOPS = 2 * BLOCKS * WINDOW * (COEFFS * OUT_BLOCKS) * SAMPLES
@@ -34,7 +32,6 @@ def tile_switchnet_fstar_pa_k_kernel(tc, x, k1, b1, grad_out, out):
     g_view = grad_out.rearrange("(c p t) a r -> c p t (a r)", p=P, t=PACK)
 
     with (
-        tc.tile_pool(name="first", bufs=1) as first_pool,
         tc.tile_pool(name="raw", bufs=6) as raw_pool,
         tc.tile_pool(name="grouped", bufs=3) as grouped_pool,
         tc.tile_pool(name="quantised", bufs=3) as quantised_pool,
@@ -63,27 +60,14 @@ def tile_switchnet_fstar_pa_k_kernel(tc, x, k1, b1, grad_out, out):
         for c in range(PASSES):
             grouped_g = grouped_pool.tile([P, WIDTH * PACK], BF16, align_bytes=64)
             grouped_x = grouped_pool.tile([P, WIDTH * PACK], BF16, align_bytes=64)
-            if c == 0:
-                for a in range(2):
-                    cols = slice(a * HALF, (a + 1) * HALF)
-                    half_x = first_pool.tile([P, PACK, HALF], BF16, name="half_x%d" % a)
-                    nc.sync.dma_start(out=half_x[:], in_=x_view[c][:, :, cols])
-                    half_g = first_pool.tile([P, PACK, HALF], BF16, name="half_g%d" % a)
-                    nc.sync.dma_start(out=half_g[:], in_=g_view[c][:, :, cols])
-                    copy_g(nc.scalar.copy, grouped_g, half_g[:], a * HALF, HALF)
-                    for h in range(2):
-                        copy_x(nc.vector.tensor_copy, grouped_x, half_x[:], a * 8, 8, h)
-            else:
+            if True:
                 raw_g = raw_pool.tile([P, PACK, WIDTH], BF16)
                 nc.sync.dma_start(out=raw_g[:], in_=g_view[c])
                 raw_x = raw_pool.tile([P, PACK, WIDTH], BF16)
                 nc.sync.dma_start(out=raw_x[:], in_=x_view[c])
                 copy_g(nc.scalar.copy, grouped_g, raw_g[:], 0, WIDTH)
                 copy_x(nc.vector.tensor_copy, grouped_x, raw_x[:], 0, GRID_ROWS, 0)
-                if c % HELP_EVERY == HELP_EVERY - 1:
-                    copy_x(nc.scalar.copy, grouped_x, raw_x[:], 0, GRID_ROWS, 1)
-                else:
-                    copy_x(nc.vector.tensor_copy, grouped_x, raw_x[:], 0, GRID_ROWS, 1)
+                copy_x(nc.vector.tensor_copy, grouped_x, raw_x[:], 0, GRID_ROWS, 1)
 
             g_codes = quantised_pool.tile([P, WIDTH], U32, align_bytes=64)
             g_scales = quantised_pool.tile([P, WIDTH], U8, align_bytes=64)

@@ -19,6 +19,7 @@ GRID_ROWS = 16
 HALF_ROW = 16
 COEFFS = 16
 OUT_BLOCKS = 8
+RAW_ALIGN = 4096
 RUN = 4
 
 FLOPS = 2 * BLOCKS * WINDOW * (COEFFS * OUT_BLOCKS) * SAMPLES
@@ -61,9 +62,9 @@ def tile_switchnet_fstar_pa_k_kernel(tc, x, k1, b1, grad_out, out):
             grouped_g = grouped_pool.tile([P, WIDTH * PACK], BF16, align_bytes=64)
             grouped_x = grouped_pool.tile([P, WIDTH * PACK], BF16, align_bytes=64)
             if True:
-                raw_g = raw_pool.tile([P, PACK, WIDTH], BF16)
+                raw_g = raw_pool.tile([P, PACK, WIDTH], BF16, align_bytes=RAW_ALIGN)
                 nc.sync.dma_start(out=raw_g[:], in_=g_view[c])
-                raw_x = raw_pool.tile([P, PACK, WIDTH], BF16)
+                raw_x = raw_pool.tile([P, PACK, WIDTH], BF16, align_bytes=RAW_ALIGN)
                 nc.sync.dma_start(out=raw_x[:], in_=x_view[c])
                 copy_g(nc.scalar.copy, grouped_g, raw_g[:], 0, WIDTH)
                 copy_x(nc.vector.tensor_copy, grouped_x, raw_x[:], 0, GRID_ROWS, 0)

@@ -20,6 +20,9 @@ HALF_ROW = 16
 COEFFS = 16
 OUT_BLOCKS = 8
 RAW_ALIGN = 4096
+X_FIRST = 16
+AHEAD = 4
+GROUPED_BUFS = 4
 RUN = 4
 
 FLOPS = 2 * BLOCKS * WINDOW * (COEFFS * OUT_BLOCKS) * SAMPLES
@@ -34,54 +37,73 @@ def tile_switchnet_fstar_pa_k_kernel(tc, x, k1, b1, grad_out, out):
 
     with (
         tc.tile_pool(name="raw", bufs=6) as raw_pool,
-        tc.tile_pool(name="grouped", bufs=3) as grouped_pool,
+        tc.tile_pool(name="grouped", bufs=GROUPED_BUFS) as grouped_pool,
         tc.tile_pool(name="quantised", bufs=3) as quantised_pool,
         tc.tile_pool(name="result", bufs=1) as result_pool,
         tc.psum_pool(name="acc", bufs=1) as acc_pool,
     ):
         acc = [acc_pool.tile([P, WIDTH], F32, name="acc%d" % j) for j in range(BLOCKS)]
         result = result_pool.tile([P, BLOCKS, OUT_BLOCKS * COEFFS], F32)
+        raws = {}
+        grouped_gs = {}
+        grouped_xs = {}
+        codes = {}
+        g_quantised = {}
 
-        def copy_g(engine_copy, grouped_g, source, first_col, cols):
-            engine_copy(
-                out=grouped_g[:, first_col * PACK : (first_col + cols) * PACK].rearrange(
-                    "p (w i t) -> p w t i", i=RUN, t=PACK
-                ),
-                in_=source.rearrange("p t (w i) -> p w t i", i=RUN),
-            )
-
-        def copy_x(engine_copy, grouped_x, source, first_row, rows, h):
-            engine_copy(
-                out=grouped_x[:].rearrange(
-                    "p (h row w i t) -> p h row w t i", h=2, row=GRID_ROWS, i=RUN, t=PACK
-                )[:, h, first_row : first_row + rows],
-                in_=source.rearrange("p t (row h w i) -> p h row w t i", row=rows, h=2, i=RUN)[:, h],
-            )
-
-        for c in range(PASSES):
-            grouped_g = grouped_pool.tile([P, WIDTH * PACK], BF16, align_bytes=64)
-            grouped_x = grouped_pool.tile([P, WIDTH * PACK], BF16, align_bytes=64)
-            if True:
-                raw_g = raw_pool.tile([P, PACK, WIDTH], BF16, align_bytes=RAW_ALIGN)
-                nc.sync.dma_start(out=raw_g[:], in_=g_view[c])
-                raw_x = raw_pool.tile([P, PACK, WIDTH], BF16, align_bytes=RAW_ALIGN)
+        def load(c):
+            raw_g = raw_pool.tile([P, PACK, WIDTH], BF16, align_bytes=RAW_ALIGN)
+            raw_x = raw_pool.tile([P, PACK, WIDTH], BF16, align_bytes=RAW_ALIGN)
+            if c < X_FIRST:
                 nc.sync.dma_start(out=raw_x[:], in_=x_view[c])
-                copy_g(nc.scalar.copy, grouped_g, raw_g[:], 0, WIDTH)
-                copy_x(nc.vector.tensor_copy, grouped_x, raw_x[:], 0, GRID_ROWS, 0)
-                copy_x(nc.vector.tensor_copy, grouped_x, raw_x[:], 0, GRID_ROWS, 1)
+                nc.sync.dma_start(out=raw_g[:], in_=g_view[c])
+            else:
+                nc.sync.dma_start(out=raw_g[:], in_=g_view[c])
+                nc.sync.dma_start(out=raw_x[:], in_=x_view[c])
+            raws[c] = (raw_g, raw_x)
 
-            g_codes = quantised_pool.tile([P, WIDTH], U32, align_bytes=64)
-            g_scales = quantised_pool.tile([P, WIDTH], U8, align_bytes=64)
+        def regroup_g(c):
+            grouped_g = grouped_pool.tile([P, WIDTH * PACK], BF16, align_bytes=64)
+            nc.scalar.copy(
+                out=grouped_g[:].rearrange("p (w i t) -> p w t i", i=RUN, t=PACK),
+                in_=raws[c][0][:].rearrange("p t (w i) -> p w t i", i=RUN),
+            )
+            grouped_gs[c] = grouped_g
+
+        def regroup_x(c):
+            grouped_x = grouped_pool.tile([P, WIDTH * PACK], BF16, align_bytes=64)
+            for h in range(2):
+                nc.vector.tensor_copy(
+                    out=grouped_x[:].rearrange(
+                        "p (h row w i t) -> p h row w t i", h=2, row=GRID_ROWS, i=RUN, t=PACK
+                    )[:, h],
+                    in_=raws[c][1][:].rearrange(
+                        "p t (row h w i) -> p h row w t i", row=GRID_ROWS, h=2, i=RUN
+                    )[:, h],
+                )
+            grouped_xs[c] = grouped_x
+
+        def quantise_x(c):
             x_codes = quantised_pool.tile([P, WIDTH], U32, align_bytes=64)
             x_scales = quantised_pool.tile([P, WIDTH], U8, align_bytes=64)
-            last = c == PASSES - 1
-            if not last:
+            codes[c] = (x_codes, x_scales)
+            if c < PASSES - 1:
                 nc.vector.quantize_mx(
-                    out=x_codes[:].bitcast(E4M3_X4), scales=x_scales[:], in_=grouped_x[:]
+                    out=x_codes[:].bitcast(E4M3_X4), scales=x_scales[:], in_=grouped_xs[c][:]
                 )
+
+        def quantise_g(c):
+            g_codes = quantised_pool.tile([P, WIDTH], U32, align_bytes=64)
+            g_scales = quantised_pool.tile([P, WIDTH], U8, align_bytes=64)
             nc.vector.quantize_mx(
-                out=g_codes[:].bitcast(E5M2_X4), scales=g_scales[:], in_=grouped_g[:]
+                out=g_codes[:].bitcast(E5M2_X4), scales=g_scales[:], in_=grouped_gs.pop(c)[:]
             )
+            g_quantised[c] = (g_codes, g_scales)
+
+        def multiply(c):
+            last = c == PASSES - 1
+            x_codes, x_scales = codes.pop(c)
+            g_codes, g_scales = g_quantised.pop(c)
+            grouped_x = grouped_xs.pop(c)
             for s in range(BLOCKS):
                 block_col, block_row = divmod(s, 2)
                 j = 2 * block_row + block_col
@@ -109,3 +131,21 @@ def tile_switchnet_fstar_pa_k_kernel(tc, x, k1, b1, grad_out, out):
                         out=result[:, j, :].rearrange("p (m r) -> p m r", m=OUT_BLOCKS), in_=picked
                     )
                     nc.sync.dma_start(out=out[j], in_=result[:, j, :])
+            raws.pop(c)
+
+        with tc.manual_schedule(engines={mybir.EngineType.DVE}):
+            for c in range(AHEAD):
+                load(c)
+            for c in range(PASSES):
+                if c + AHEAD < PASSES:
+                    load(c + AHEAD)
+                regroup_g(c)
+                regroup_x(c)
+                if 0 < c <= X_FIRST:
+                    quantise_g(c - 1)
+                    multiply(c - 1)
+                if c >= X_FIRST:
+                    quantise_g(c)
+                quantise_x(c)
+                if c >= X_FIRST:
+                    multiply(c)

@@ -23,6 +23,7 @@ RAW_ALIGN = 4096
 X_FIRST = 16
 AHEAD = 4
 GROUPED_BUFS = 4
+HELPED = (31,)
 RUN = 4
 
 FLOPS = 2 * BLOCKS * WINDOW * (COEFFS * OUT_BLOCKS) * SAMPLES
@@ -72,7 +73,8 @@ def tile_switchnet_fstar_pa_k_kernel(tc, x, k1, b1, grad_out, out):
         def regroup_x(c):
             grouped_x = grouped_pool.tile([P, WIDTH * PACK], BF16, align_bytes=64)
             for h in range(2):
-                nc.vector.tensor_copy(
+                copy = nc.scalar.copy if h == 1 and c in HELPED else nc.vector.tensor_copy
+                copy(
                     out=grouped_x[:].rearrange(
                         "p (h row w i t) -> p h row w t i", h=2, row=GRID_ROWS, i=RUN, t=PACK
                     )[:, h],

import concourse.mybir as mybir

BF16 = mybir.dt.bfloat16
F32 = mybir.dt.float32
U32 = mybir.dt.uint32
U8 = mybir.dt.uint8
E4M3_X4 = mybir.dt.float8_e4m3fn_x4
E5M2_X4 = mybir.dt.float8_e5m2_x4

P = 128
PACK = 4
K_PASS = P * PACK
SAMPLES = 16384
PASSES = SAMPLES // K_PASS
WIDTH = 512
BLOCKS = 4
WINDOW = 128
GRID_ROWS = 16
HALF_ROW = 16
COEFFS = 16
OUT_BLOCKS = 8
RAW_ALIGN = 4096
X_FIRST = 16
AHEAD = 4
GROUPED_BUFS = 4
HELPED = (31,)
RUN = 4

FLOPS = 2 * BLOCKS * WINDOW * (COEFFS * OUT_BLOCKS) * SAMPLES
BYTES = 2 * SAMPLES * WIDTH * 2 + BLOCKS * WINDOW * COEFFS * OUT_BLOCKS * 4


def tile_switchnet_fstar_pa_k_kernel(tc, x, k1, b1, grad_out, out):
    nc = tc.nc

    x_view = x.rearrange("(c p t) g ch -> c p t (g ch)", p=P, t=PACK)
    g_view = grad_out.rearrange("(c p t) a r -> c p t (a r)", p=P, t=PACK)

    with (
        tc.tile_pool(name="raw", bufs=6) as raw_pool,
        tc.tile_pool(name="grouped", bufs=GROUPED_BUFS) as grouped_pool,
        tc.tile_pool(name="quantised", bufs=3) as quantised_pool,
        tc.tile_pool(name="result", bufs=1) as result_pool,
        tc.psum_pool(name="acc", bufs=1) as acc_pool,
    ):
        acc = [acc_pool.tile([P, WIDTH], F32, name="acc%d" % j) for j in range(BLOCKS)]
        result = result_pool.tile([P, BLOCKS, OUT_BLOCKS * COEFFS], F32)
        raws = {}
        grouped_gs = {}
        grouped_xs = {}
        codes = {}
        g_quantised = {}

        def load(c):
            raw_g = raw_pool.tile([P, PACK, WIDTH], BF16, align_bytes=RAW_ALIGN)
            raw_x = raw_pool.tile([P, PACK, WIDTH], BF16, align_bytes=RAW_ALIGN)
            if c < X_FIRST:
                nc.sync.dma_start(out=raw_x[:], in_=x_view[c])
                nc.sync.dma_start(out=raw_g[:], in_=g_view[c])
            else:
                nc.sync.dma_start(out=raw_g[:], in_=g_view[c])
                nc.sync.dma_start(out=raw_x[:], in_=x_view[c])
            raws[c] = (raw_g, raw_x)

        def regroup_g(c):
            grouped_g = grouped_pool.tile([P, WIDTH * PACK], BF16, align_bytes=64)
            nc.scalar.copy(
                out=grouped_g[:].rearrange("p (w i t) -> p w t i", i=RUN, t=PACK),
                in_=raws[c][0][:].rearrange("p t (w i) -> p w t i", i=RUN),
            )
            grouped_gs[c] = grouped_g

        def regroup_x(c):
            grouped_x = grouped_pool.tile([P, WIDTH * PACK], BF16, align_bytes=64)
            for h in range(2):
                copy = nc.scalar.copy if h == 1 and c in HELPED else nc.vector.tensor_copy
                copy(
                    out=grouped_x[:].rearrange(
                        "p (h row w i t) -> p h row w t i", h=2, row=GRID_ROWS, i=RUN, t=PACK
                    )[:, h],
                    in_=raws[c][1][:].rearrange(
                        "p t (row h w i) -> p h row w t i", row=GRID_ROWS, h=2, i=RUN
                    )[:, h],
                )
            grouped_xs[c] = grouped_x

        def quantise_x(c):
            x_codes = quantised_pool.tile([P, WIDTH], U32, align_bytes=64)
            x_scales = quantised_pool.tile([P, WIDTH], U8, align_bytes=64)
            codes[c] = (x_codes, x_scales)
            if c < PASSES - 1:
                nc.vector.quantize_mx(
                    out=x_codes[:].bitcast(E4M3_X4), scales=x_scales[:], in_=grouped_xs[c][:]
                )

        def quantise_g(c):
            g_codes = quantised_pool.tile([P, WIDTH], U32, align_bytes=64)
            g_scales = quantised_pool.tile([P, WIDTH], U8, align_bytes=64)
            nc.vector.quantize_mx(
                out=g_codes[:].bitcast(E5M2_X4), scales=g_scales[:], in_=grouped_gs.pop(c)[:]
            )
            g_quantised[c] = (g_codes, g_scales)

        def multiply(c):
            last = c == PASSES - 1
            x_codes, x_scales = codes.pop(c)
            g_codes, g_scales = g_quantised.pop(c)
            grouped_x = grouped_xs.pop(c)
            for s in range(BLOCKS):
                block_col, block_row = divmod(s, 2)
                j = 2 * block_row + block_col
                cols = slice(s * WINDOW, (s + 1) * WINDOW)
                if last:
                    nc.vector.quantize_mx(
                        out=x_codes[:, cols].bitcast(E4M3_X4),
                        scales=x_scales[:, cols],
                        in_=grouped_x[:, s * WINDOW * PACK : (s + 1) * WINDOW * PACK],
                    )
                nc.tensor.matmul_mx(
                    out=acc[j][:],
                    lhsT=x_codes[:, cols].bitcast(E4M3_X4),
                    lhsT_scale=x_scales[:, cols],
                    rhs=g_codes[:].bitcast(E5M2_X4),
                    rhs_scale=g_scales[:],
                    start=(c == 0),
                    stop=last,
                )
                if last:
                    picked = acc[j][:].rearrange(
                        "p (r j m) -> p j m r", r=COEFFS, j=BLOCKS, m=OUT_BLOCKS
                    )[:, j]
                    nc.scalar.copy(
                        out=result[:, j, :].rearrange("p (m r) -> p m r", m=OUT_BLOCKS), in_=picked
                    )
                    nc.sync.dma_start(out=out[j], in_=result[:, j, :])
            raws.pop(c)

        with tc.manual_schedule(engines={mybir.EngineType.DVE}):
            for c in range(AHEAD):
                load(c)
            for c in range(PASSES):
                if c + AHEAD < PASSES:
                    load(c + AHEAD)
                regroup_g(c)
                regroup_x(c)
                if 0 < c <= X_FIRST:
                    quantise_g(c - 1)
                    multiply(c - 1)
                if c >= X_FIRST:
                    quantise_g(c)
                quantise_x(c)
                if c >= X_FIRST:
                    multiply(c)
